import numpy as np
import ml_dtypes


def mxq(x, axis, fmt="e4m3"):
    dtype, down = {"e4m3": (ml_dtypes.float8_e4m3fn, 7), "e5m2": (ml_dtypes.float8_e5m2, 14)}[fmt]
    v = np.moveaxis(np.asarray(x, np.float32).astype(ml_dtypes.bfloat16).astype(np.float64), axis, -1)
    blocks = v.reshape(v.shape[:-1] + (-1, 32))
    amax = np.abs(blocks).max(-1, keepdims=True)
    byte = np.maximum(np.where(amax > 0, np.frexp(amax)[1] - 1 + 127, 0) - down, 1)
    scale = np.exp2(byte - 127.0)
    codes = (blocks / scale).astype(np.float32).astype(dtype).astype(np.float64)
    return np.moveaxis((codes * scale).reshape(v.shape), -1, axis)


WIDE = False


def mx_kscale(k):
    if not WIDE:
        return np.ones(k)
    levels = np.array([10, -10, 5, -5, 0])
    if k % 512:
        return np.exp2(np.random.permutation(np.resize(levels, k // 32))).repeat(32)
    a = np.empty((k // 512, 16))
    for p in range(k // 512):
        a[p, :8] = np.random.permutation(np.resize(levels, 8))
        for g in range(8):
            far = levels[np.abs(levels - a[p, g]) >= 10]
            a[p, g + 8] = far[np.random.randint(len(far))]
    return np.exp2(a.ravel()).repeat(32)


BF16 = ml_dtypes.bfloat16


def bf(x):
    return np.asarray(x, np.float32).astype(BF16)


def f64(x):
    return np.asarray(x).astype(np.float64)


B, DIM = 2048, 1024


def setup_inputs():
    s = mx_kscale(DIM)
    p = np.random.standard_normal((B, DIM)) / s
    q = np.random.standard_normal((B, DIM)) * s
    A = np.random.standard_normal((DIM, DIM)) * 0.7 / np.sqrt(DIM) / s[:, None] / s[None, :]
    return {"pq": bf(np.concatenate([p, q], axis=1)), "A": bf(A)}


def reference(pq, A):
    pq, A = f64(pq), f64(A)
    S = A + A.T
    p = pq[..., :DIM]
    q = pq[..., DIM:]
    pterm = mxq(q, 1, "e4m3") @ mxq(S, 1, "e4m3").T
    return np.concatenate([p + pterm, q], axis=-1)

@@ -1,0 +1,224 @@
+from contextlib import ExitStack
+
+import concourse.mybir as mybir
+from concourse.masks import make_identity
+
+FLOPS = 2 * 2048 * 1024 * 1024
+
+F32 = mybir.dt.float32
+BF16 = mybir.dt.bfloat16
+U32 = mybir.dt.uint32
+U8 = mybir.dt.uint8
+FP8X4 = mybir.dt.float8_e4m3fn_x4
+ADD = mybir.AluOpType.add
+
+P = 128
+B = 2048
+DIM = 1024
+T = B // P
+CHUNK_T = 4
+PAIRS = T // 2
+O_BUFS = 6
+
+
+def tile_linear_sub_kernel(tc, pq, A, out):
+    nc = tc.nc
+    with ExitStack() as ctx:
+        keep = ctx.enter_context(tc.tile_pool(name="keep", bufs=1))
+        qpool = ctx.enter_context(tc.tile_pool(name="qpool", bufs=3))
+        opool = ctx.enter_context(tc.tile_pool(name="opool", bufs=O_BUFS))
+        tpsum = ctx.enter_context(tc.psum_pool(name="tpsum", bufs=4))
+        apsum = ctx.enter_context(tc.psum_pool(name="apsum", bufs=4))
+        ctx.enter_context(tc.manual_schedule())
+
+        pq_v = pq.rearrange("(p t) c -> p t c", t=T)
+        out_v = out.rearrange("(p t) c -> p t c", t=T)
+        a_v = A.rearrange("(g p t) c -> g p (t c)", g=2, p=P, t=4)
+
+        a_sb = []
+        for g in range(2):
+            a_t = keep.tile([P, 4 * DIM], BF16, name="a_sb%d" % g)
+            nc.sync.dma_start(out=a_t[:], in_=a_v[g])
+            a_sb.append(a_t)
+        pq_sb = []
+        for i in range(T // CHUNK_T):
+            pq_t = keep.tile([P, CHUNK_T * 2 * DIM], BF16, name="pq_sb%d" % i)
+            nc.sync.dma_start(
+                out=pq_t[:].rearrange("p (t c) -> p t c", t=CHUNK_T),
+                in_=pq_v[:, CHUNK_T * i : CHUNK_T * (i + 1), :],
+            )
+            pq_sb.append(pq_t)
+
+        ident = keep.tile([P, P], F32, name="ident")
+        make_identity(nc, ident[:])
+
+        s_grp = []
+        s_codes = []
+        s_scl = []
+        for g in range(2):
+            s_grp.append(keep.tile([P, 4 * DIM], BF16, name="s_grp%d" % g, align_bytes=64))
+            s_codes.append(keep.tile([P, DIM], U32, name="s_codes%d" % g, align_bytes=64))
+            s_scl.append(keep.tile([P, DIM], U8, name="s_scl%d" % g, align_bytes=64))
+
+        at_tiles = {}
+        qt_tiles = {}
+        state = {}
+
+        def a_transposes(n):
+            g, jc = divmod(n, 4)
+            at_ps = tpsum.tile([P, 512], F32, name="at_ps", tag="tp")
+            a_w = a_sb[jc // 2][:].bitcast(F32)
+            for ec in range(2):
+                for u in range(2):
+                    w0 = (2 * (jc % 2) + ec) * 512 + 256 * g + u
+                    pos = ec * 2 + u
+                    nc.tensor.transpose(
+                        out=at_ps[:, 128 * pos : 128 * pos + 128],
+                        in_=a_w[:, w0 : w0 + 255 : 2],
+                        identity=ident[:],
+                    )
+            at_tiles[n] = at_ps
+
+        def s_add(n):
+            g, jc = divmod(n, 4)
+            nc.vector.tensor_tensor(
+                out=s_grp[g][:, 2048 * (jc // 2) : 2048 * (jc // 2) + 2048].rearrange(
+                    "p (pc tp ec u e) -> p tp pc ec u e", pc=P, tp=2, ec=2, u=2, e=2
+                )[:, jc % 2],
+                in0=at_tiles[n][:].bitcast(BF16).rearrange(
+                    "p (ec u pc e) -> p pc ec u e", ec=2, u=2, pc=P, e=2
+                ),
+                in1=a_sb[g][:]
+                .rearrange("p (u e c) -> p u e c", u=2, e=2)[:, :, :, 512 * (jc // 2) : 512 * (jc // 2) + 512]
+                .rearrange("p u e (pc tp ec) -> p tp pc ec u e", tp=2, ec=2)[:, jc % 2],
+                op=ADD,
+            )
+
+        def s_quantise(g, h):
+            nc.vector.quantize_mx(
+                out=s_codes[g][:, 512 * h : 512 * h + 512].bitcast(FP8X4),
+                scales=s_scl[g][:, 512 * h : 512 * h + 512],
+                in_=s_grp[g][:, 2048 * h : 2048 * h + 2048],
+            )
+
+        def q_transposes(k):
+            pq_w = pq_sb[k // 2][:].bitcast(F32)
+            banks = []
+            for tt in range(2):
+                t4 = 2 * (k % 2) + tt
+                qt_ps = tpsum.tile([P, 512], F32, name="qt_ps", tag="tp")
+                for jw in range(4):
+                    w0 = t4 * 1024 + 512 + 256 * (jw // 2) + jw % 2
+                    nc.tensor.transpose(
+                        out=qt_ps[:, 128 * jw : 128 * jw + 128],
+                        in_=pq_w[:, w0 : w0 + 255 : 2],
+                        identity=ident[:],
+                    )
+                banks.append(qt_ps)
+            qt_tiles[k] = banks
+
+        def q_copies(k):
+            pq_t = pq_sb[k // 2]
+            o_sb = opool.tile([P, 2 * 2 * DIM], F32, name="o_sb")
+            q_grp = qpool.tile([P, 2048], BF16, name="q_grp", align_bytes=64)
+            q_grp_w = q_grp[:].bitcast(F32)
+            for tt in range(2):
+                nc.scalar.copy(
+                    out=q_grp_w[:, 512 * tt : 512 * tt + 512].rearrange(
+                        "p (g b u) -> p g b u", g=2, b=P, u=2
+                    ),
+                    in_=qt_tiles[k][tt][:].rearrange("p (g u b) -> p g b u", g=2, u=2, b=P),
+                )
+            t0 = 2 * (k % 2)
+            nc.scalar.copy(
+                out=o_sb[:].rearrange("p (t c) -> p t c", t=2)[:, :, DIM : 2 * DIM],
+                in_=pq_t[:].rearrange("p (t c) -> p t c", t=CHUNK_T)[:, t0 : t0 + 2, DIM : 2 * DIM],
+            )
+            state[k] = [o_sb, q_grp]
+
+        def q_quantise(k):
+            q_c = qpool.tile([P, 512], U32, name="q_codes", align_bytes=64)
+            q_s = qpool.tile([P, 512], U8, name="q_scl", align_bytes=64)
+            nc.vector.quantize_mx(out=q_c[:].bitcast(FP8X4), scales=q_s[:], in_=state[k][1][:])
+            state[k].extend([q_c, q_s])
+
+        def passes(k):
+            q_c, q_s = state[k][2], state[k][3]
+            accs = []
+            for tt in range(2):
+                for h in range(2):
+                    acc = apsum.tile([P, 512], F32, name="acc")
+                    for g in range(2):
+                        c0 = 256 * tt + 128 * g
+                        nc.tensor.matmul_mx(
+                            out=acc[:],
+                            lhsT=q_c[:, c0 : c0 + 128].bitcast(FP8X4),
+                            lhsT_scale=q_s[:, c0 : c0 + 128],
+                            rhs=s_codes[g][:, 512 * h : 512 * h + 512].bitcast(FP8X4),
+                            rhs_scale=s_scl[g][:, 512 * h : 512 * h + 512],
+                            start=(g == 0),
+                            stop=(g == 1),
+                        )
+                    accs.append(acc)
+            state[k].append(accs)
+
+        def p_adds(k, tt):
+            pq_t = pq_sb[k // 2]
+            o_sb = state[k][0]
+            t4 = 2 * (k % 2) + tt
+            for h in range(2):
+                nc.vector.tensor_tensor(
+                    out=o_sb[:, 2048 * tt + 512 * h : 2048 * tt + 512 * h + 512],
+                    in0=state[k][4][2 * tt + h][:],
+                    in1=pq_t[:, 2048 * t4 + 512 * h : 2048 * t4 + 512 * h + 512],
+                    op=ADD,
+                )
+
+        def store(k, tt0, tt1):
+            nc.sync.dma_start(
+                out=out_v[:, 2 * k + tt0 : 2 * k + tt1, :],
+                in_=state[k][0][:].rearrange("p (t c) -> p t c", t=2)[:, tt0:tt1, :],
+            )
+
+        for n in range(4):
+            a_transposes(n)
+        s_add(0)
+        s_add(1)
+        a_transposes(4)
+        a_transposes(5)
+        s_add(2)
+        s_quantise(0, 0)
+        s_add(3)
+        q_transposes(0)
+        q_copies(0)
+        s_add(4)
+        s_quantise(0, 1)
+        s_add(5)
+        a_transposes(6)
+        a_transposes(7)
+        s_add(6)
+        s_quantise(1, 0)
+        s_add(7)
+        q_transposes(1)
+        q_copies(1)
+        q_transposes(2)
+        q_copies(2)
+        q_quantise(0)
+        s_quantise(1, 1)
+        passes(0)
+        p_adds(0, 0)
+        store(0, 0, 1)
+        q_quantise(1)
+        p_adds(0, 1)
+        store(0, 1, 2)
+        q_quantise(2)
+        for k in range(1, PAIRS):
+            if k + 2 < PAIRS:
+                q_transposes(k + 2)
+                q_copies(k + 2)
+            passes(k)
+            p_adds(k, 0)
+            p_adds(k, 1)
+            store(k, 0, 2)
+            if k + 2 < PAIRS:
+                q_quantise(k + 2)

@@ -37,12 +37,12 @@ def tile_linear_sub_kernel(tc, pq, A, out):
 
         a_sb = []
         for g in range(2):
-            a_t = keep.tile([P, 4 * DIM], BF16, name="a_sb%d" % g)
+            a_t = keep.tile([P, 4 * DIM], BF16, name="a_sb%d" % g, align_bytes=256)
             nc.sync.dma_start(out=a_t[:], in_=a_v[g])
             a_sb.append(a_t)
         pq_sb = []
         for i in range(T // CHUNK_T):
-            pq_t = keep.tile([P, CHUNK_T * 2 * DIM], BF16, name="pq_sb%d" % i)
+            pq_t = keep.tile([P, CHUNK_T * 2 * DIM], BF16, name="pq_sb%d" % i, align_bytes=256)
             nc.sync.dma_start(
                 out=pq_t[:].rearrange("p (t c) -> p t c", t=CHUNK_T),
                 in_=pq_v[:, CHUNK_T * i : CHUNK_T * (i + 1), :],
@@ -119,7 +119,7 @@ def tile_linear_sub_kernel(tc, pq, A, out):
 
         def q_copies(k):
             pq_t = pq_sb[k // 2]
-            o_sb = opool.tile([P, 2 * 2 * DIM], F32, name="o_sb")
+            o_sb = opool.tile([P, 2 * 2 * DIM], F32, name="o_sb", align_bytes=256)
             q_grp = qpool.tile([P, 2048], BF16, name="q_grp", align_bytes=64)
             q_grp_w = q_grp[:].bitcast(F32)
             for tt in range(2):

@@ -16,9 +16,9 @@ P = 128
 B = 2048
 DIM = 1024
 T = B // P
-CHUNK_T = 4
 PAIRS = T // 2
-O_BUFS = 6
+LOAD_TILES = (4, 6, 6)
+STORE_PAIRS = (1, 1, 1, 1, 2, 2)
 
 
 def tile_linear_sub_kernel(tc, pq, A, out):
@@ -26,7 +26,7 @@ def tile_linear_sub_kernel(tc, pq, A, out):
     with ExitStack() as ctx:
         keep = ctx.enter_context(tc.tile_pool(name="keep", bufs=1))
         qpool = ctx.enter_context(tc.tile_pool(name="qpool", bufs=3))
-        opool = ctx.enter_context(tc.tile_pool(name="opool", bufs=O_BUFS))
+        opool = ctx.enter_context(tc.tile_pool(name="opool", bufs=1))
         tpsum = ctx.enter_context(tc.psum_pool(name="tpsum", bufs=4))
         apsum = ctx.enter_context(tc.psum_pool(name="apsum", bufs=4))
         ctx.enter_context(tc.manual_schedule())
@@ -35,42 +35,63 @@ def tile_linear_sub_kernel(tc, pq, A, out):
         out_v = out.rearrange("(p t) c -> p t c", t=T)
         a_v = A.rearrange("(g p t) c -> g p (t c)", g=2, p=P, t=4)
 
+        work = opool.tile([P, 16 * DIM], BF16, name="work", tag="o_long", bufs=2, align_bytes=256)
         a_sb = []
+        s_grp = []
         for g in range(2):
-            a_t = keep.tile([P, 4 * DIM], BF16, name="a_sb%d" % g, align_bytes=256)
-            nc.sync.dma_start(out=a_t[:], in_=a_v[g])
-            a_sb.append(a_t)
-        pq_sb = []
-        for i in range(T // CHUNK_T):
-            pq_t = keep.tile([P, CHUNK_T * 2 * DIM], BF16, name="pq_sb%d" % i, align_bytes=256)
+            a_sb.append(work[:, 4 * DIM * g : 4 * DIM * (g + 1)])
+            s_grp.append(work[:, 4 * DIM * (2 + g) : 4 * DIM * (3 + g)])
+            nc.sync.dma_start(out=a_sb[g], in_=a_v[g])
+        pq_rows = []
+        for i, tiles in enumerate(LOAD_TILES):
+            pq_t = keep.tile([P, tiles * 2 * DIM], BF16, name="pq_sb%d" % i, align_bytes=256)
+            t0 = len(pq_rows)
             nc.sync.dma_start(
-                out=pq_t[:].rearrange("p (t c) -> p t c", t=CHUNK_T),
-                in_=pq_v[:, CHUNK_T * i : CHUNK_T * (i + 1), :],
+                out=pq_t[:].rearrange("p (t c) -> p t c", t=tiles),
+                in_=pq_v[:, t0 : t0 + tiles, :],
             )
-            pq_sb.append(pq_t)
+            pq_rows.extend([pq_t[:, 2 * DIM * t : 2 * DIM * (t + 1)] for t in range(tiles)])
 
         ident = keep.tile([P, P], F32, name="ident")
         make_identity(nc, ident[:])
 
-        s_grp = []
         s_codes = []
         s_scl = []
         for g in range(2):
-            s_grp.append(keep.tile([P, 4 * DIM], BF16, name="s_grp%d" % g, align_bytes=64))
             s_codes.append(keep.tile([P, DIM], U32, name="s_codes%d" % g, align_bytes=64))
             s_scl.append(keep.tile([P, DIM], U8, name="s_scl%d" % g, align_bytes=64))
 
         at_tiles = {}
         qt_tiles = {}
-        state = {}
+        q_grps = {}
+        q_mx = {}
+        accs = {}
+        o_rows = {}
+        stores = {}
+
+        first = 0
+        for pairs in STORE_PAIRS:
+            kind = "o_short" if pairs == 1 else "o_long"
+            o_t = opool.tile(
+                [P, 4 * DIM * pairs],
+                F32,
+                name="%s%d" % (kind, first),
+                tag=kind,
+                bufs=4 if pairs == 1 else 2,
+                align_bytes=256,
+            )
+            for t in range(2 * pairs):
+                o_rows[2 * first + t] = o_t[:, 2 * DIM * t : 2 * DIM * (t + 1)]
+            stores[first + pairs - 1] = (first, pairs, o_t)
+            first += pairs
 
         def a_transposes(n):
-            g, jc = divmod(n, 4)
-            at_ps = tpsum.tile([P, 512], F32, name="at_ps", tag="tp")
-            a_w = a_sb[jc // 2][:].bitcast(F32)
+            g, j = divmod(n, 4)
+            at_ps = apsum.tile([P, 512], F32, name="at_ps", tag="acc")
+            a_w = a_sb[j // 2].bitcast(F32)
             for ec in range(2):
                 for u in range(2):
-                    w0 = (2 * (jc % 2) + ec) * 512 + 256 * g + u
+                    w0 = (2 * (j % 2) + ec) * 512 + 256 * g + u
                     pos = ec * 2 + u
                     nc.tensor.transpose(
                         out=at_ps[:, 128 * pos : 128 * pos + 128],
@@ -80,17 +101,18 @@ def tile_linear_sub_kernel(tc, pq, A, out):
             at_tiles[n] = at_ps
 
         def s_add(n):
-            g, jc = divmod(n, 4)
+            g, j = divmod(n, 4)
+            h, tp = divmod(j, 2)
             nc.vector.tensor_tensor(
-                out=s_grp[g][:, 2048 * (jc // 2) : 2048 * (jc // 2) + 2048].rearrange(
+                out=s_grp[g][:, 2048 * h : 2048 * h + 2048].rearrange(
                     "p (pc tp ec u e) -> p tp pc ec u e", pc=P, tp=2, ec=2, u=2, e=2
-                )[:, jc % 2],
+                )[:, tp],
                 in0=at_tiles[n][:].bitcast(BF16).rearrange(
                     "p (ec u pc e) -> p pc ec u e", ec=2, u=2, pc=P, e=2
                 ),
-                in1=a_sb[g][:]
-                .rearrange("p (u e c) -> p u e c", u=2, e=2)[:, :, :, 512 * (jc // 2) : 512 * (jc // 2) + 512]
-                .rearrange("p u e (pc tp ec) -> p tp pc ec u e", tp=2, ec=2)[:, jc % 2],
+                in1=a_sb[g]
+                .rearrange("p (u e c) -> p u e c", u=2, e=2)[:, :, :, 512 * h : 512 * h + 512]
+                .rearrange("p u e (pc tp ec) -> p tp pc ec u e", tp=2, ec=2)[:, tp],
                 op=ADD,
             )
 
@@ -102,24 +124,21 @@ def tile_linear_sub_kernel(tc, pq, A, out):
             )
 
         def q_transposes(k):
-            pq_w = pq_sb[k // 2][:].bitcast(F32)
-            banks = []
+            qt_tiles[k] = []
             for tt in range(2):
-                t4 = 2 * (k % 2) + tt
-                qt_ps = tpsum.tile([P, 512], F32, name="qt_ps", tag="tp")
-                for jw in range(4):
-                    w0 = t4 * 1024 + 512 + 256 * (jw // 2) + jw % 2
-                    nc.tensor.transpose(
-                        out=qt_ps[:, 128 * jw : 128 * jw + 128],
-                        in_=pq_w[:, w0 : w0 + 255 : 2],
-                        identity=ident[:],
-                    )
-                banks.append(qt_ps)
-            qt_tiles[k] = banks
+                q_w = pq_rows[2 * k + tt][:, DIM : 2 * DIM].bitcast(F32)
+                qt_ps = tpsum.tile([P, 512], F32, name="qt_ps")
+                for g in range(2):
+                    for u in range(2):
+                        c0 = 256 * g + 128 * u
+                        nc.tensor.transpose(
+                            out=qt_ps[:, c0 : c0 + 128],
+                            in_=q_w[:, 256 * g + u : 256 * g + u + 255 : 2],
+                            identity=ident[:],
+                        )
+                qt_tiles[k].append(qt_ps)
 
         def q_copies(k):
-            pq_t = pq_sb[k // 2]
-            o_sb = opool.tile([P, 2 * 2 * DIM], F32, name="o_sb", align_bytes=256)
             q_grp = qpool.tile([P, 2048], BF16, name="q_grp", align_bytes=64)
             q_grp_w = q_grp[:].bitcast(F32)
             for tt in range(2):
@@ -129,25 +148,23 @@ def tile_linear_sub_kernel(tc, pq, A, out):
                     ),
                     in_=qt_tiles[k][tt][:].rearrange("p (g u b) -> p g b u", g=2, u=2, b=P),
                 )
-            t0 = 2 * (k % 2)
-            nc.scalar.copy(
-                out=o_sb[:].rearrange("p (t c) -> p t c", t=2)[:, :, DIM : 2 * DIM],
-                in_=pq_t[:].rearrange("p (t c) -> p t c", t=CHUNK_T)[:, t0 : t0 + 2, DIM : 2 * DIM],
-            )
-            state[k] = [o_sb, q_grp]
+            q_grps[k] = q_grp
+
+        def q_casts(k):
+            for t in (2 * k, 2 * k + 1):
+                nc.scalar.copy(out=o_rows[t][:, DIM : 2 * DIM], in_=pq_rows[t][:, DIM : 2 * DIM])
 
         def q_quantise(k):
             q_c = qpool.tile([P, 512], U32, name="q_codes", align_bytes=64)
             q_s = qpool.tile([P, 512], U8, name="q_scl", align_bytes=64)
-            nc.vector.quantize_mx(out=q_c[:].bitcast(FP8X4), scales=q_s[:], in_=state[k][1][:])
-            state[k].extend([q_c, q_s])
+            nc.vector.quantize_mx(out=q_c[:].bitcast(FP8X4), scales=q_s[:], in_=q_grps[k][:])
+            q_mx[k] = (q_c, q_s)
 
         def passes(k):
-            q_c, q_s = state[k][2], state[k][3]
-            accs = []
+            q_c, q_s = q_mx[k]
             for tt in range(2):
                 for h in range(2):
-                    acc = apsum.tile([P, 512], F32, name="acc")
+                    acc = apsum.tile([P, 512], F32, name="acc", tag="acc")
                     for g in range(2):
                         c0 = 256 * tt + 128 * g
                         nc.tensor.matmul_mx(
@@ -159,66 +176,58 @@ def tile_linear_sub_kernel(tc, pq, A, out):
                             start=(g == 0),
                             stop=(g == 1),
                         )
-                    accs.append(acc)
-            state[k].append(accs)
+                    accs[2 * k + tt, h] = acc
 
-        def p_adds(k, tt):
-            pq_t = pq_sb[k // 2]
-            o_sb = state[k][0]
-            t4 = 2 * (k % 2) + tt
-            for h in range(2):
-                nc.vector.tensor_tensor(
-                    out=o_sb[:, 2048 * tt + 512 * h : 2048 * tt + 512 * h + 512],
-                    in0=state[k][4][2 * tt + h][:],
-                    in1=pq_t[:, 2048 * t4 + 512 * h : 2048 * t4 + 512 * h + 512],
-                    op=ADD,
+        def p_adds(k):
+            for t in (2 * k, 2 * k + 1):
+                for h in range(2):
+                    cols = slice(512 * h, 512 * h + 512)
+                    nc.vector.tensor_tensor(
+                        out=o_rows[t][:, cols],
+                        in0=accs[t, h][:],
+                        in1=pq_rows[t][:, cols],
+                        op=ADD,
+                    )
+
+        def store(k):
+            if k in stores:
+                first_pair, pairs, o_t = stores[k]
+                nc.sync.dma_start(
+                    out=out_v[:, 2 * first_pair : 2 * (first_pair + pairs), :],
+                    in_=o_t[:].rearrange("p (t c) -> p t c", t=2 * pairs),
                 )
 
-        def store(k, tt0, tt1):
-            nc.sync.dma_start(
-                out=out_v[:, 2 * k + tt0 : 2 * k + tt1, :],
-                in_=state[k][0][:].rearrange("p (t c) -> p t c", t=2)[:, tt0:tt1, :],
-            )
-
-        for n in range(4):
+        for n in range(8):
             a_transposes(n)
-        s_add(0)
-        s_add(1)
-        a_transposes(4)
-        a_transposes(5)
-        s_add(2)
-        s_quantise(0, 0)
-        s_add(3)
+            if n == 3:
+                s_add(0)
+                s_add(1)
+                s_add(2)
+                s_quantise(0, 0)
+                s_add(3)
+            elif n == 7:
+                s_add(4)
+                s_quantise(0, 1)
+                s_add(5)
+                s_add(6)
+                s_quantise(1, 0)
+                s_add(7)
         q_transposes(0)
         q_copies(0)
-        s_add(4)
-        s_quantise(0, 1)
-        s_add(5)
-        a_transposes(6)
-        a_transposes(7)
-        s_add(6)
-        s_quantise(1, 0)
-        s_add(7)
         q_transposes(1)
         q_copies(1)
-        q_transposes(2)
-        q_copies(2)
+        q_casts(0)
+        q_casts(1)
         q_quantise(0)
         s_quantise(1, 1)
-        passes(0)
-        p_adds(0, 0)
-        store(0, 0, 1)
         q_quantise(1)
-        p_adds(0, 1)
-        store(0, 1, 2)
-        q_quantise(2)
-        for k in range(1, PAIRS):
+        for k in range(PAIRS):
+            passes(k)
             if k + 2 < PAIRS:
                 q_transposes(k + 2)
                 q_copies(k + 2)
-            passes(k)
-            p_adds(k, 0)
-            p_adds(k, 1)
-            store(k, 0, 2)
+                q_casts(k + 2)
+            p_adds(k)
+            store(k)
             if k + 2 < PAIRS:
                 q_quantise(k + 2)

@@ -17,8 +17,8 @@ B = 2048
 DIM = 1024
 T = B // P
 PAIRS = T // 2
-LOAD_TILES = (4, 6, 6)
-STORE_PAIRS = (1, 1, 1, 1, 2, 2)
+LOAD_TILES = (4, 4, 4, 4)
+STORE_PAIRS = (1, 2, 2, 2, 1)
 
 
 def tile_linear_sub_kernel(tc, pq, A, out):
@@ -35,7 +35,9 @@ def tile_linear_sub_kernel(tc, pq, A, out):
         out_v = out.rearrange("(p t) c -> p t c", t=T)
         a_v = A.rearrange("(g p t) c -> g p (t c)", g=2, p=P, t=4)
 
-        work = opool.tile([P, 16 * DIM], BF16, name="work", tag="o_long", bufs=2, align_bytes=256)
+        work = opool.tile(
+            [P, 16 * DIM], BF16, name="work", tag="o_2", bufs=STORE_PAIRS.count(2), align_bytes=256
+        )
         a_sb = []
         s_grp = []
         for g in range(2):
@@ -69,15 +71,18 @@ def tile_linear_sub_kernel(tc, pq, A, out):
         o_rows = {}
         stores = {}
 
+        a_int = opool.tile(
+            [P, 8 * DIM], BF16, name="a_int", tag="o_1", bufs=STORE_PAIRS.count(1), align_bytes=256
+        )
+
         first = 0
         for pairs in STORE_PAIRS:
-            kind = "o_short" if pairs == 1 else "o_long"
             o_t = opool.tile(
                 [P, 4 * DIM * pairs],
                 F32,
-                name="%s%d" % (kind, first),
-                tag=kind,
-                bufs=4 if pairs == 1 else 2,
+                name="o_rows%d" % first,
+                tag="o_%d" % pairs,
+                bufs=STORE_PAIRS.count(pairs),
                 align_bytes=256,
             )
             for t in range(2 * pairs):
@@ -100,6 +105,15 @@ def tile_linear_sub_kernel(tc, pq, A, out):
                     )
             at_tiles[n] = at_ps
 
+        def a_interleave(copy, g, h):
+            c0 = 4 * DIM * g + 2048 * h
+            copy(
+                out=a_int[:, c0 : c0 + 2048].rearrange("p (pc i t) -> p pc t i", i=4, t=4),
+                in_=a_sb[g].rearrange("p (t c) -> p t c", t=4)[:, :, 512 * h : 512 * h + 512].rearrange(
+                    "p t (pc i) -> p pc t i", i=4
+                ),
+            )
+
         def s_add(n):
             g, j = divmod(n, 4)
             h, tp = divmod(j, 2)
@@ -110,9 +124,9 @@ def tile_linear_sub_kernel(tc, pq, A, out):
                 in0=at_tiles[n][:].bitcast(BF16).rearrange(
                     "p (ec u pc e) -> p pc ec u e", ec=2, u=2, pc=P, e=2
                 ),
-                in1=a_sb[g]
-                .rearrange("p (u e c) -> p u e c", u=2, e=2)[:, :, :, 512 * h : 512 * h + 512]
-                .rearrange("p u e (pc tp ec) -> p tp pc ec u e", tp=2, ec=2)[:, tp],
+                in1=a_int[:, 4 * DIM * g + 2048 * h : 4 * DIM * g + 2048 * h + 2048].rearrange(
+                    "p (pc tp ec u e) -> p tp pc ec u e", pc=P, tp=2, ec=2, u=2, e=2
+                )[:, tp],
                 op=ADD,
             )
 
@@ -197,6 +211,9 @@ def tile_linear_sub_kernel(tc, pq, A, out):
                     in_=o_t[:].rearrange("p (t c) -> p t c", t=2 * pairs),
                 )
 
+        a_interleave(nc.vector.tensor_copy, 0, 0)
+        a_interleave(nc.scalar.copy, 0, 1)
+        a_interleave(nc.scalar.copy, 1, 1)
         for n in range(8):
             a_transposes(n)
             if n == 3:
@@ -205,9 +222,10 @@ def tile_linear_sub_kernel(tc, pq, A, out):
                 s_add(2)
                 s_quantise(0, 0)
                 s_add(3)
+                a_interleave(nc.vector.tensor_copy, 1, 0)
+                s_quantise(0, 1)
             elif n == 7:
                 s_add(4)
-                s_quantise(0, 1)
                 s_add(5)
                 s_add(6)
                 s_quantise(1, 0)

@@ -17,8 +17,8 @@ B = 2048
 DIM = 1024
 T = B // P
 PAIRS = T // 2
-LOAD_TILES = (4, 4, 4, 4)
-STORE_PAIRS = (1, 2, 2, 2, 1)
+LOAD_TILES = (4, 4, 8)
+STORE_PAIRS = (1, 2, 2, 3)
 
 
 def tile_linear_sub_kernel(tc, pq, A, out):
@@ -33,7 +33,7 @@ def tile_linear_sub_kernel(tc, pq, A, out):
 
         pq_v = pq.rearrange("(p t) c -> p t c", t=T)
         out_v = out.rearrange("(p t) c -> p t c", t=T)
-        a_v = A.rearrange("(g p t) c -> g p (t c)", g=2, p=P, t=4)
+        a_v = A.rearrange("(g p t) c -> p g (t c)", g=2, p=P, t=4)
 
         work = opool.tile(
             [P, 16 * DIM], BF16, name="work", tag="o_2", bufs=STORE_PAIRS.count(2), align_bytes=256
@@ -43,7 +43,9 @@ def tile_linear_sub_kernel(tc, pq, A, out):
         for g in range(2):
             a_sb.append(work[:, 4 * DIM * g : 4 * DIM * (g + 1)])
             s_grp.append(work[:, 4 * DIM * (2 + g) : 4 * DIM * (3 + g)])
-            nc.sync.dma_start(out=a_sb[g], in_=a_v[g])
+        nc.sync.dma_start(
+            out=work[:, 0 : 8 * DIM].rearrange("p (g x) -> p g x", g=2), in_=a_v
+        )
         pq_rows = []
         for i, tiles in enumerate(LOAD_TILES):
             pq_t = keep.tile([P, tiles * 2 * DIM], BF16, name="pq_sb%d" % i, align_bytes=256)
@@ -72,7 +74,7 @@ def tile_linear_sub_kernel(tc, pq, A, out):
         stores = {}
 
         a_int = opool.tile(
-            [P, 8 * DIM], BF16, name="a_int", tag="o_1", bufs=STORE_PAIRS.count(1), align_bytes=256
+            [P, 8 * DIM], BF16, name="a_int", tag="o_3", bufs=STORE_PAIRS.count(3), align_bytes=256
         )
 
         first = 0
@@ -235,16 +237,19 @@ def tile_linear_sub_kernel(tc, pq, A, out):
         q_transposes(1)
         q_copies(1)
         q_casts(0)
-        q_casts(1)
+        q_transposes(2)
+        q_copies(2)
         q_quantise(0)
         s_quantise(1, 1)
         q_quantise(1)
         for k in range(PAIRS):
+            if k + 1 < PAIRS:
+                q_casts(k + 1)
             passes(k)
-            if k + 2 < PAIRS:
-                q_transposes(k + 2)
-                q_copies(k + 2)
-                q_casts(k + 2)
+            for n in {0: (3,), 1: (), 2: (4, 5)}.get(k, (k + 3,)):
+                if n < PAIRS:
+                    q_transposes(n)
+                    q_copies(n)
             p_adds(k)
             store(k)
             if k + 2 < PAIRS:

@@ -17,8 +17,8 @@ B = 2048
 DIM = 1024
 T = B // P
 PAIRS = T // 2
-LOAD_TILES = (4, 4, 8)
-STORE_PAIRS = (1, 2, 2, 3)
+LOAD_TILES = (6, 10)
+STORE_TILES = (2, 3, 3, 4, 4)
 
 
 def tile_linear_sub_kernel(tc, pq, A, out):
@@ -35,9 +35,7 @@ def tile_linear_sub_kernel(tc, pq, A, out):
         out_v = out.rearrange("(p t) c -> p t c", t=T)
         a_v = A.rearrange("(g p t) c -> p g (t c)", g=2, p=P, t=4)
 
-        work = opool.tile(
-            [P, 16 * DIM], BF16, name="work", tag="o_2", bufs=STORE_PAIRS.count(2), align_bytes=256
-        )
+        work = opool.tile([P, 16 * DIM], BF16, name="work", tag="o_rows3", align_bytes=256)
         a_sb = []
         s_grp = []
         for g in range(2):
@@ -73,24 +71,16 @@ def tile_linear_sub_kernel(tc, pq, A, out):
         o_rows = {}
         stores = {}
 
-        a_int = opool.tile(
-            [P, 8 * DIM], BF16, name="a_int", tag="o_3", bufs=STORE_PAIRS.count(3), align_bytes=256
-        )
+        a_int = opool.tile([P, 8 * DIM], BF16, name="a_int", tag="o_rows4", align_bytes=256)
 
         first = 0
-        for pairs in STORE_PAIRS:
-            o_t = opool.tile(
-                [P, 4 * DIM * pairs],
-                F32,
-                name="o_rows%d" % first,
-                tag="o_%d" % pairs,
-                bufs=STORE_PAIRS.count(pairs),
-                align_bytes=256,
-            )
-            for t in range(2 * pairs):
-                o_rows[2 * first + t] = o_t[:, 2 * DIM * t : 2 * DIM * (t + 1)]
-            stores[first + pairs - 1] = (first, pairs, o_t)
-            first += pairs
+        for i, tiles in enumerate(STORE_TILES):
+            name = "o_rows%d" % i
+            o_t = opool.tile([P, 2 * DIM * tiles], F32, name=name, tag=name, align_bytes=256)
+            for t in range(tiles):
+                o_rows[first + t] = o_t[:, 2 * DIM * t : 2 * DIM * (t + 1)]
+            stores[first + tiles - 1] = (first, tiles, o_t)
+            first += tiles
 
         def a_transposes(n):
             g, j = divmod(n, 4)
@@ -194,7 +184,7 @@ def tile_linear_sub_kernel(tc, pq, A, out):
                         )
                     accs[2 * k + tt, h] = acc
 
-        def p_adds(k):
+        def p_adds_and_stores(k):
             for t in (2 * k, 2 * k + 1):
                 for h in range(2):
                     cols = slice(512 * h, 512 * h + 512)
@@ -204,14 +194,12 @@ def tile_linear_sub_kernel(tc, pq, A, out):
                         in1=pq_rows[t][:, cols],
                         op=ADD,
                     )
-
-        def store(k):
-            if k in stores:
-                first_pair, pairs, o_t = stores[k]
-                nc.sync.dma_start(
-                    out=out_v[:, 2 * first_pair : 2 * (first_pair + pairs), :],
-                    in_=o_t[:].rearrange("p (t c) -> p t c", t=2 * pairs),
-                )
+                if t in stores:
+                    first_tile, tiles, o_t = stores[t]
+                    nc.sync.dma_start(
+                        out=out_v[:, first_tile : first_tile + tiles, :],
+                        in_=o_t[:].rearrange("p (t c) -> p t c", t=tiles),
+                    )
 
         a_interleave(nc.vector.tensor_copy, 0, 0)
         a_interleave(nc.scalar.copy, 0, 1)
@@ -243,14 +231,20 @@ def tile_linear_sub_kernel(tc, pq, A, out):
         s_quantise(1, 1)
         q_quantise(1)
         for k in range(PAIRS):
+            passes(k)
+            if k < 2:
+                coming = ()
+            elif k == 2:
+                coming = (3, 4)
+            else:
+                coming = range(k + 2, min(k + 3, PAIRS))
+            for n in coming:
+                q_transposes(n)
+                q_copies(n)
             if k + 1 < PAIRS:
                 q_casts(k + 1)
-            passes(k)
-            for n in {0: (3,), 1: (), 2: (4, 5)}.get(k, (k + 3,)):
-                if n < PAIRS:
-                    q_transposes(n)
-                    q_copies(n)
-            p_adds(k)
-            store(k)
-            if k + 2 < PAIRS:
-                q_quantise(k + 2)
+            p_adds_and_stores(k)
+            if k == 0:
+                q_quantise(2)
+            for n in coming:
+                q_quantise(n)

from contextlib import ExitStack

import concourse.mybir as mybir
from concourse.masks import make_identity

FLOPS = 2 * 2048 * 1024 * 1024

F32 = mybir.dt.float32
BF16 = mybir.dt.bfloat16
U32 = mybir.dt.uint32
U8 = mybir.dt.uint8
FP8X4 = mybir.dt.float8_e4m3fn_x4
ADD = mybir.AluOpType.add

P = 128
B = 2048
DIM = 1024
T = B // P
PAIRS = T // 2
LOAD_TILES = (6, 10)
STORE_TILES = (2, 3, 3, 4, 4)


def tile_linear_sub_kernel(tc, pq, A, out):
    nc = tc.nc
    with ExitStack() as ctx:
        keep = ctx.enter_context(tc.tile_pool(name="keep", bufs=1))
        qpool = ctx.enter_context(tc.tile_pool(name="qpool", bufs=3))
        opool = ctx.enter_context(tc.tile_pool(name="opool", bufs=1))
        tpsum = ctx.enter_context(tc.psum_pool(name="tpsum", bufs=4))
        apsum = ctx.enter_context(tc.psum_pool(name="apsum", bufs=4))
        ctx.enter_context(tc.manual_schedule())

        pq_v = pq.rearrange("(p t) c -> p t c", t=T)
        out_v = out.rearrange("(p t) c -> p t c", t=T)
        a_v = A.rearrange("(g p t) c -> p g (t c)", g=2, p=P, t=4)

        work = opool.tile([P, 16 * DIM], BF16, name="work", tag="o_rows3", align_bytes=256)
        a_sb = []
        s_grp = []
        for g in range(2):
            a_sb.append(work[:, 4 * DIM * g : 4 * DIM * (g + 1)])
            s_grp.append(work[:, 4 * DIM * (2 + g) : 4 * DIM * (3 + g)])
        nc.sync.dma_start(
            out=work[:, 0 : 8 * DIM].rearrange("p (g x) -> p g x", g=2), in_=a_v
        )
        pq_rows = []
        for i, tiles in enumerate(LOAD_TILES):
            pq_t = keep.tile([P, tiles * 2 * DIM], BF16, name="pq_sb%d" % i, align_bytes=256)
            t0 = len(pq_rows)
            nc.sync.dma_start(
                out=pq_t[:].rearrange("p (t c) -> p t c", t=tiles),
                in_=pq_v[:, t0 : t0 + tiles, :],
            )
            pq_rows.extend([pq_t[:, 2 * DIM * t : 2 * DIM * (t + 1)] for t in range(tiles)])

        ident = keep.tile([P, P], F32, name="ident")
        make_identity(nc, ident[:])

        s_codes = []
        s_scl = []
        for g in range(2):
            s_codes.append(keep.tile([P, DIM], U32, name="s_codes%d" % g, align_bytes=64))
            s_scl.append(keep.tile([P, DIM], U8, name="s_scl%d" % g, align_bytes=64))

        at_tiles = {}
        qt_tiles = {}
        q_grps = {}
        q_mx = {}
        accs = {}
        o_rows = {}
        stores = {}

        a_int = opool.tile([P, 8 * DIM], BF16, name="a_int", tag="o_rows4", align_bytes=256)

        first = 0
        for i, tiles in enumerate(STORE_TILES):
            name = "o_rows%d" % i
            o_t = opool.tile([P, 2 * DIM * tiles], F32, name=name, tag=name, align_bytes=256)
            for t in range(tiles):
                o_rows[first + t] = o_t[:, 2 * DIM * t : 2 * DIM * (t + 1)]
            stores[first + tiles - 1] = (first, tiles, o_t)
            first += tiles

        def a_transposes(n):
            g, j = divmod(n, 4)
            at_ps = apsum.tile([P, 512], F32, name="at_ps", tag="acc")
            a_w = a_sb[j // 2].bitcast(F32)
            for ec in range(2):
                for u in range(2):
                    w0 = (2 * (j % 2) + ec) * 512 + 256 * g + u
                    pos = ec * 2 + u
                    nc.tensor.transpose(
                        out=at_ps[:, 128 * pos : 128 * pos + 128],
                        in_=a_w[:, w0 : w0 + 255 : 2],
                        identity=ident[:],
                    )
            at_tiles[n] = at_ps

        def a_interleave(copy, g, h):
            c0 = 4 * DIM * g + 2048 * h
            copy(
                out=a_int[:, c0 : c0 + 2048].rearrange("p (pc i t) -> p pc t i", i=4, t=4),
                in_=a_sb[g].rearrange("p (t c) -> p t c", t=4)[:, :, 512 * h : 512 * h + 512].rearrange(
                    "p t (pc i) -> p pc t i", i=4
                ),
            )

        def s_add(n):
            g, j = divmod(n, 4)
            h, tp = divmod(j, 2)
            nc.vector.tensor_tensor(
                out=s_grp[g][:, 2048 * h : 2048 * h + 2048].rearrange(
                    "p (pc tp ec u e) -> p tp pc ec u e", pc=P, tp=2, ec=2, u=2, e=2
                )[:, tp],
                in0=at_tiles[n][:].bitcast(BF16).rearrange(
                    "p (ec u pc e) -> p pc ec u e", ec=2, u=2, pc=P, e=2
                ),
                in1=a_int[:, 4 * DIM * g + 2048 * h : 4 * DIM * g + 2048 * h + 2048].rearrange(
                    "p (pc tp ec u e) -> p tp pc ec u e", pc=P, tp=2, ec=2, u=2, e=2
                )[:, tp],
                op=ADD,
            )

        def s_quantise(g, h):
            nc.vector.quantize_mx(
                out=s_codes[g][:, 512 * h : 512 * h + 512].bitcast(FP8X4),
                scales=s_scl[g][:, 512 * h : 512 * h + 512],
                in_=s_grp[g][:, 2048 * h : 2048 * h + 2048],
            )

        def q_transposes(k):
            qt_tiles[k] = []
            for tt in range(2):
                q_w = pq_rows[2 * k + tt][:, DIM : 2 * DIM].bitcast(F32)
                qt_ps = tpsum.tile([P, 512], F32, name="qt_ps")
                for g in range(2):
                    for u in range(2):
                        c0 = 256 * g + 128 * u
                        nc.tensor.transpose(
                            out=qt_ps[:, c0 : c0 + 128],
                            in_=q_w[:, 256 * g + u : 256 * g + u + 255 : 2],
                            identity=ident[:],
                        )
                qt_tiles[k].append(qt_ps)

        def q_copies(k):
            q_grp = qpool.tile([P, 2048], BF16, name="q_grp", align_bytes=64)
            q_grp_w = q_grp[:].bitcast(F32)
            for tt in range(2):
                nc.scalar.copy(
                    out=q_grp_w[:, 512 * tt : 512 * tt + 512].rearrange(
                        "p (g b u) -> p g b u", g=2, b=P, u=2
                    ),
                    in_=qt_tiles[k][tt][:].rearrange("p (g u b) -> p g b u", g=2, u=2, b=P),
                )
            q_grps[k] = q_grp

        def q_casts(k):
            for t in (2 * k, 2 * k + 1):
                nc.scalar.copy(out=o_rows[t][:, DIM : 2 * DIM], in_=pq_rows[t][:, DIM : 2 * DIM])

        def q_quantise(k):
            q_c = qpool.tile([P, 512], U32, name="q_codes", align_bytes=64)
            q_s = qpool.tile([P, 512], U8, name="q_scl", align_bytes=64)
            nc.vector.quantize_mx(out=q_c[:].bitcast(FP8X4), scales=q_s[:], in_=q_grps[k][:])
            q_mx[k] = (q_c, q_s)

        def passes(k):
            q_c, q_s = q_mx[k]
            for tt in range(2):
                for h in range(2):
                    acc = apsum.tile([P, 512], F32, name="acc", tag="acc")
                    for g in range(2):
                        c0 = 256 * tt + 128 * g
                        nc.tensor.matmul_mx(
                            out=acc[:],
                            lhsT=q_c[:, c0 : c0 + 128].bitcast(FP8X4),
                            lhsT_scale=q_s[:, c0 : c0 + 128],
                            rhs=s_codes[g][:, 512 * h : 512 * h + 512].bitcast(FP8X4),
                            rhs_scale=s_scl[g][:, 512 * h : 512 * h + 512],
                            start=(g == 0),
                            stop=(g == 1),
                        )
                    accs[2 * k + tt, h] = acc

        def p_adds_and_stores(k):
            for t in (2 * k, 2 * k + 1):
                for h in range(2):
                    cols = slice(512 * h, 512 * h + 512)
                    nc.vector.tensor_tensor(
                        out=o_rows[t][:, cols],
                        in0=accs[t, h][:],
                        in1=pq_rows[t][:, cols],
                        op=ADD,
                    )
                if t in stores:
                    first_tile, tiles, o_t = stores[t]
                    nc.sync.dma_start(
                        out=out_v[:, first_tile : first_tile + tiles, :],
                        in_=o_t[:].rearrange("p (t c) -> p t c", t=tiles),
                    )

        a_interleave(nc.vector.tensor_copy, 0, 0)
        a_interleave(nc.scalar.copy, 0, 1)
        a_interleave(nc.scalar.copy, 1, 1)
        for n in range(8):
            a_transposes(n)
            if n == 3:
                s_add(0)
                s_add(1)
                s_add(2)
                s_quantise(0, 0)
                s_add(3)
                a_interleave(nc.vector.tensor_copy, 1, 0)
                s_quantise(0, 1)
            elif n == 7:
                s_add(4)
                s_add(5)
                s_add(6)
                s_quantise(1, 0)
                s_add(7)
        q_transposes(0)
        q_copies(0)
        q_transposes(1)
        q_copies(1)
        q_casts(0)
        q_transposes(2)
        q_copies(2)
        q_quantise(0)
        s_quantise(1, 1)
        q_quantise(1)
        for k in range(PAIRS):
            passes(k)
            if k < 2:
                coming = ()
            elif k == 2:
                coming = (3, 4)
            else:
                coming = range(k + 2, min(k + 3, PAIRS))
            for n in coming:
                q_transposes(n)
                q_copies(n)
            if k + 1 < PAIRS:
                q_casts(k + 1)
            p_adds_and_stores(k)
            if k == 0:
                q_quantise(2)
            for n in coming:
                q_quantise(n)
